import numpy as np
import ml_dtypes


def mxq(x, axis, fmt="e4m3"):
    dtype, down = {"e4m3": (ml_dtypes.float8_e4m3fn, 7), "e5m2": (ml_dtypes.float8_e5m2, 14)}[fmt]
    v = np.moveaxis(np.asarray(x, np.float32).astype(ml_dtypes.bfloat16).astype(np.float64), axis, -1)
    blocks = v.reshape(v.shape[:-1] + (-1, 32))
    amax = np.abs(blocks).max(-1, keepdims=True)
    byte = np.maximum(np.where(amax > 0, np.frexp(amax)[1] - 1 + 127, 0) - down, 1)
    scale = np.exp2(byte - 127.0)
    codes = (blocks / scale).astype(np.float32).astype(dtype).astype(np.float64)
    return np.moveaxis((codes * scale).reshape(v.shape), -1, axis)


WIDE = False


def mx_kscale(k):
    if not WIDE:
        return np.ones(k)
    levels = np.array([30, -30])
    if k % 512:
        return np.exp2(np.random.permutation(np.resize(levels, k // 32))).repeat(32)
    a = np.empty((k // 512, 16))
    for p in range(k // 512):
        a[p, :8] = np.random.permutation(np.resize(levels, 8))
        for g in range(8):
            far = levels[np.abs(levels - a[p, g]) >= 10]
            a[p, g + 8] = far[np.random.randint(len(far))]
    return np.exp2(a.ravel()).repeat(32)


BF16 = ml_dtypes.bfloat16


def bf(x):
    return np.asarray(x, np.float32).astype(BF16)


def f64(x):
    return np.asarray(x).astype(np.float64)


E2M1 = np.array([0.0, 0.5, 1.0, 1.5, 2.0, 3.0, 4.0, 6.0, -0.0, -0.5, -1.0, -1.5, -2.0, -3.0, -4.0, -6.0])


def pack_weight(w, fmt):
    k, n = w.shape
    w = f64(bf(w)).reshape(k // 32, 32, n)
    amax = np.abs(w).max(1)
    if fmt == "e4m3":
        byte = np.frexp(amax)[1] - 1 + 127 - 7
    else:
        mant, ex = np.frexp(amax / 6.0)
        byte = np.where(mant > 0.5, ex, ex - 1) + 127
    byte = np.clip(np.where(amax > 0, byte, 1), 1, 254)
    scaled = (w * np.exp2(127.0 - byte)[:, None, :]).reshape(k, n).astype(np.float32)
    by_word = np.ascontiguousarray(scaled.reshape(k // 512, 128, 4, n).transpose(0, 1, 3, 2))
    if fmt == "e4m3":
        words = by_word.astype(ml_dtypes.float8_e4m3fn).view(np.uint8)
    else:
        c = by_word.astype(ml_dtypes.float4_e2m1fn).view(np.uint8) & 0xF
        words = c[..., 0::2] | (c[..., 1::2] << 4)
    return np.ascontiguousarray(words), np.ascontiguousarray(byte.astype(np.uint8).reshape(k // 512, 16, n))


def unpack_weight(words, scales, fmt):
    g, p, n, _ = words.shape
    if fmt == "e4m3":
        vals = np.ascontiguousarray(words).view(ml_dtypes.float8_e4m3fn).astype(np.float64)
    else:
        nib = np.empty((g, p, n, 4), np.uint8)
        nib[..., 0::2] = words & 0xF
        nib[..., 1::2] = words >> 4
        vals = E2M1[nib]
    vals = vals * np.repeat(np.exp2(scales.astype(np.float64) - 127.0), 8, axis=1)[..., None]
    return vals.transpose(0, 1, 3, 2).reshape(g * 512, n)

def pack4(w):
    words, scales = pack_weight(w, "e2m1")
    return words.reshape(words.shape[0], 128, -1), scales


def unpack4(words, scales):
    return unpack_weight(words.reshape(words.shape[0], 128, -1, 2), scales, "e2m1")


B, S, H, D = 2, 512, 16, 64
E = H * D
HALF = D // 2


def rotate_half(u):
    u1, u2 = np.split(u, 2, axis=-1)
    return np.concatenate([-u2, u1], axis=-1)


def apply_rope(t, sin, cos):
    x1, x2 = np.split(t, 2, axis=-1)
    x_rot = x1 * cos + rotate_half(x1) * sin
    return np.concatenate([x_rot, x2], axis=-1)


def setup_inputs():
    s = mx_kscale(E)
    th = np.random.uniform(0.0, 2.0 * np.pi, (S, HALF))
    x = bf(np.random.standard_normal((B, S, E)) * s)
    words, scales = pack4(np.random.standard_normal((E, 3 * E)) / np.sqrt(E) / s[:, None])
    return {"x": x,
            "W_qkv_words": words,
            "W_qkv_scales": scales,
            "b_qkv": bf(np.random.standard_normal(3 * E) * 0.2),
            "sin_tab": bf(np.sin(th)),
            "cos_tab": bf(np.cos(th))}


def reference(x, W_qkv_words, W_qkv_scales, b_qkv, sin_tab, cos_tab):
    qkv = (mxq(f64(x), 2, "e5m2") @ unpack4(W_qkv_words, W_qkv_scales)) + f64(b_qkv)
    q, k, v = np.split(qkv, 3, axis=-1)
    q = q.reshape(B, S, H, D)
    k = k.reshape(B, S, H, D)
    v = v.reshape(B, S, H, D)
    sin = f64(sin_tab)[None, :, None, :]
    cos = f64(cos_tab)[None, :, None, :]
    q_rot = apply_rope(q, sin, cos)
    k_rot = apply_rope(k, sin, cos)
    return q_rot, k_rot, v

@@ -1,0 +1,226 @@
+from contextlib import ExitStack
+
+import concourse.mybir as mybir
+from concourse.masks import make_identity
+
+B, S, H, D = 2, 512, 16, 64
+E = H * D
+ROT = D // 2
+PAIR = ROT // 2
+FLOPS = 2 * B * S * E * 3 * E
+
+F32 = mybir.dt.float32
+BF16 = mybir.dt.bfloat16
+I32 = mybir.dt.int32
+U32 = mybir.dt.uint32
+U8 = mybir.dt.uint8
+E5M2X4 = mybir.dt.float8_e5m2_x4
+E2M1X4 = mybir.dt.float4_e2m1fn_x4
+ALU = mybir.AluOpType
+ACT = mybir.ActivationFunctionType
+
+P = 128
+PASSES = E // 512
+BANK = 512
+CHUNKS = 3 * E // BANK
+QK_CHUNKS = 2 * E // BANK
+HEADS_PER_BANK = BANK // D
+POS_TILES = S // P
+TILES = B * POS_TILES
+QK_HEADS = 2 * H
+W_LOADS = [(0, 1), (1, 2), (2, 4), (4, 6)]
+POOL_COS = 4
+BIAS_ROWS = 2
+BIAS_CHUNKS = CHUNKS // BIAS_ROWS
+
+
+def tile_improvedattention_pa_kernel(tc, x, W_qkv_words, W_qkv_scales, b_qkv, sin_tab, cos_tab, out_0, out_1, out_2):
+    nc = tc.nc
+
+    def token_rows(ap, i):
+        return ap[i % B].rearrange("(p t) e -> t p e", t=POS_TILES)[i // B]
+
+    outs = [o.rearrange("b s h d -> b s (h d)") for o in (out_0, out_1, out_2)]
+
+    with ExitStack() as ctx:
+        keep = ctx.enter_context(tc.tile_pool(name="keep", bufs=1))
+        work = ctx.enter_context(tc.tile_pool(name="work", bufs=3))
+        stage = ctx.enter_context(tc.tile_pool(name="stage", bufs=4))
+        psum = ctx.enter_context(tc.psum_pool(name="psum", bufs=8))
+        ctx.enter_context(tc.manual_schedule())
+
+        ident = keep.tile([P, P], F32, name="ident")
+        pick = keep.tile([P, 8], BF16, name="pick")
+        bias_rows = keep.tile([P, BIAS_CHUNKS * BANK], BF16, name="bias_rows")
+        w_scale = keep.tile([P, PASSES, 3 * E], U8, name="w_scale", align_bytes=64)
+        cos_raw = keep.tile([P, POS_TILES, ROT], BF16, name="cos_raw")
+        sin_raw = keep.tile([P, POS_TILES, ROT], BF16, name="sin_raw")
+        cos = keep.tile([P, POS_TILES, ROT], F32, name="cos")
+        sin = keep.tile([P, POS_TILES, ROT], F32, name="sin")
+        bias_rot = [keep.tile([P, ROT, HEADS_PER_BANK], F32, name="bias_rot%d" % c) for c in range(QK_CHUNKS)]
+        bias_pass = [keep.tile([P, HEADS_PER_BANK, ROT], F32, name="bias_pass%d" % c) for c in range(QK_CHUNKS)]
+        bias_v = [keep.tile([P, BANK], F32, name="bias_v%d" % c) for c in range(CHUNKS - QK_CHUNKS)]
+        x_sb = [keep.tile([P, E], BF16, name="x%d" % i) for i in range(TILES)]
+        codes = [keep.tile([P, PASSES * P], U32, name="codes%d" % i, align_bytes=64) for i in range(TILES)]
+        x_scale = [keep.tile([P, PASSES * P], U8, name="xscale%d" % i, align_bytes=64) for i in range(TILES)]
+        w_words = {}
+        x_t, grouped, turned, plain, value, t_cos, t_sin = {}, {}, {}, {}, {}, {}, {}
+
+        def load_x(i):
+            nc.sync.dma_start(out=x_sb[i][:], in_=token_rows(x, i))
+
+        def load_w(c0, c1):
+            w = keep.tile([P, PASSES, 2 * BANK * (c1 - c0)], U8, name="w%d" % c0, align_bytes=64)
+            src = W_qkv_words[:, :, 2 * BANK * c0 : 2 * BANK * c1].rearrange("g p n -> p g n")
+            nc.sync.dma_start(out=w[:].bitcast(I32), in_=src.bitcast(I32))
+            for c in range(c0, c1):
+                w_words[c] = w[:, :, 2 * BANK * (c - c0) : 2 * BANK * (c - c0 + 1)]
+
+        def transpose_x(i):
+            xt = psum.tile([P, PASSES, 2, P], F32, name="xt", tag="bank")
+            words = x_sb[i][:].bitcast(F32)
+            for g in range(PASSES):
+                for u in range(2):
+                    nc.tensor.transpose(xt[:, g, u, :], words[:, 256 * g + u : 256 * (g + 1) : 2], ident[:])
+            x_t[i] = xt
+
+        def group_x(i):
+            gr = work.tile([P, E], BF16, name="gr", align_bytes=64)
+            nc.scalar.copy(
+                out=gr[:].bitcast(F32).rearrange("p (g r u) -> p g r u", g=PASSES, u=2),
+                in_=x_t[i][:].rearrange("p g u r -> p g r u"),
+            )
+            grouped[i] = gr
+
+        def quantize_x(i):
+            nc.vector.quantize_mx(out=codes[i][:].bitcast(E5M2X4), scales=x_scale[i][:], in_=grouped[i][:])
+
+        def spread_bias(c, copy):
+            row, part = divmod(c, BIAS_CHUNKS)
+            acc = psum.tile([P, BANK], F32, name="bias_acc", tag="bank")
+            nc.tensor.matmul(acc[:], lhsT=pick[:, row : row + 1].to_broadcast([P, P]), rhs=bias_rows[:, BANK * part : BANK * (part + 1)], start=True, stop=True)
+            if c < QK_CHUNKS:
+                copy(out=bias_rot[c][:], in_=acc[:].rearrange("p (h d) -> p d h", d=D)[:, 0:ROT, :])
+                copy(out=bias_pass[c][:], in_=acc[:].rearrange("p (h d) -> p h d", d=D)[:, :, ROT:D])
+            else:
+                copy(out=bias_v[c - QK_CHUNKS][:], in_=acc[:])
+
+        def project(i, c):
+            if c == 0:
+                plain[i] = work.tile([P, ROT, QK_HEADS], F32, name="u")
+                turned[i] = stage.tile([P, QK_HEADS, D], F32, name="qk")
+                value[i] = stage.tile([P, E], F32, name="v")
+            acc = psum.tile([P, BANK], F32, name="acc", tag="bank")
+            for g in range(PASSES):
+                nc.tensor.matmul_mx(
+                    out=acc[:],
+                    lhsT=codes[i][:, P * g : P * (g + 1)].bitcast(E5M2X4),
+                    lhsT_scale=x_scale[i][:, P * g : P * (g + 1)],
+                    rhs=w_words[c][:, g, :].bitcast(E2M1X4),
+                    rhs_scale=w_scale[:, g, BANK * c : BANK * (c + 1)],
+                    start=(g == 0),
+                    stop=(g == PASSES - 1),
+                )
+            if c < QK_CHUNKS:
+                heads = slice(HEADS_PER_BANK * c, HEADS_PER_BANK * (c + 1))
+                nc.vector.tensor_tensor(
+                    out=plain[i][:, :, heads],
+                    in0=acc[:].rearrange("p (h d) -> p d h", d=D)[:, 0:ROT, :],
+                    in1=bias_rot[c][:],
+                    op=ALU.add,
+                )
+                nc.vector.tensor_tensor(
+                    out=turned[i][:, heads, ROT:D],
+                    in0=acc[:].rearrange("p (h d) -> p h d", d=D)[:, :, ROT:D],
+                    in1=bias_pass[c][:],
+                    op=ALU.add,
+                )
+            else:
+                cv = c - QK_CHUNKS
+                nc.vector.tensor_tensor(out=value[i][:, BANK * cv : BANK * (cv + 1)], in0=acc[:], in1=bias_v[cv][:], op=ALU.add)
+
+        def cos_share(i):
+            t_cos[i] = work.tile([P, ROT, QK_HEADS], F32, name="t_cos")
+            t_sin[i] = work.tile([P, ROT, QK_HEADS], F32, name="t_sin")
+            js = slice(ROT - POOL_COS, ROT)
+            nc.gpsimd.tensor_tensor(
+                out=t_cos[i][:, js, :],
+                in0=plain[i][:, js, :],
+                in1=cos[:, i // B, js].unsqueeze(2).to_broadcast([P, POOL_COS, QK_HEADS]),
+                op=ALU.mult,
+            )
+
+        def rotate(i, half):
+            t = i // B
+            for j in range(PAIR * half, PAIR * (half + 1)):
+                mate = (j + PAIR) % ROT
+                if j < ROT - POOL_COS:
+                    nc.scalar.activation(out=t_cos[i][:, j, :], in_=plain[i][:, j, :], func=ACT.Copy, scale=cos[:, t, j : j + 1])
+                nc.scalar.activation(out=t_sin[i][:, j, :], in_=plain[i][:, mate, :], func=ACT.Copy, scale=sin[:, t, j : j + 1])
+            js = slice(PAIR * half, PAIR * (half + 1))
+            nc.gpsimd.tensor_tensor(
+                out=turned[i][:, :, js].rearrange("p n (a j) -> p a n j", j=4),
+                in0=t_cos[i][:, js, :].rearrange("p (a j) n -> p a n j", j=4),
+                in1=t_sin[i][:, js, :].rearrange("p (a j) n -> p a n j", j=4),
+                op=ALU.subtract if half == 0 else ALU.add,
+            )
+
+        def store_qk(i):
+            for k in range(2):
+                nc.sync.dma_start(out=token_rows(outs[k], i), in_=turned[i][:, H * k : H * (k + 1), :].rearrange("p h d -> p (h d)"))
+
+        def store_v(i):
+            nc.sync.dma_start(out=token_rows(outs[2], i), in_=value[i][:])
+
+        make_identity(nc, ident[:])
+        nc.gpsimd.tensor_copy(out=pick[:], in_=ident[:, 0:8])
+        nc.vector.memset(bias_rows[:].bitcast(I32), 0)
+        nc.vector.memset(w_scale[:].bitcast(I32), 0)
+        nc.scalar.dma_start(out=bias_rows[0:BIAS_ROWS, :], in_=b_qkv.rearrange("(r n) -> r n", r=BIAS_ROWS))
+        nc.scalar.dma_start(out=cos_raw[:], in_=cos_tab.rearrange("(p t) j -> p t j", t=POS_TILES))
+        nc.scalar.dma_start(out=sin_raw[:], in_=sin_tab.rearrange("(p t) j -> p t j", t=POS_TILES))
+        load_x(0)
+        for q in range(4):
+            nc.sync.dma_start(
+                out=w_scale[32 * q : 32 * q + 4, :, :].bitcast(I32),
+                in_=W_qkv_scales[:, 4 * q : 4 * q + 4, :].rearrange("g r n -> r g n").bitcast(I32),
+            )
+        for c0, c1 in W_LOADS[:3]:
+            load_w(c0, c1)
+        load_x(1)
+        load_w(*W_LOADS[3])
+        for i in range(2, TILES):
+            load_x(i)
+        nc.scalar.activation(out=cos[:], in_=cos_raw[:], func=ACT.Copy)
+        nc.scalar.activation(out=sin[:], in_=sin_raw[:], func=ACT.Copy)
+
+        transpose_x(0)
+        group_x(0)
+        quantize_x(0)
+        spread_bias(0, nc.vector.tensor_copy)
+        spread_bias(1, nc.scalar.copy)
+
+        for i in range(TILES):
+            ahead = [n for n in (i + 2, i + 3) if i % 2 == 0 and n < TILES]
+            for c in range(CHUNKS):
+                if i == 0 and c == QK_CHUNKS:
+                    transpose_x(1)
+                    group_x(1)
+                project(i, c)
+                if i == 0 and c + 2 < CHUNKS:
+                    spread_bias(c + 2, nc.scalar.copy)
+                if i == 0 and c == QK_CHUNKS:
+                    quantize_x(1)
+                if i % 2 == 1 and c == 2:
+                    for n in (i + 1, i + 2):
+                        if n < TILES:
+                            quantize_x(n)
+            store_v(i)
+            for n in ahead:
+                transpose_x(n)
+            cos_share(i)
+            rotate(i, 0)
+            for n in ahead:
+                group_x(n)
+            rotate(i, 1)
+            store_qk(i)

@@ -29,7 +29,9 @@ POS_TILES = S // P
 TILES = B * POS_TILES
 QK_HEADS = 2 * H
 W_LOADS = [(0, 1), (1, 2), (2, 4), (4, 6)]
-POOL_COS = 4
+LINE = 4
+GROUPS = PAIR // LINE
+VEC_COS = PAIR - LINE
 BIAS_ROWS = 2
 BIAS_CHUNKS = CHUNKS // BIAS_ROWS
 
@@ -57,14 +59,12 @@ def tile_improvedattention_pa_kernel(tc, x, W_qkv_words, W_qkv_scales, b_qkv, si
         sin_raw = keep.tile([P, POS_TILES, ROT], BF16, name="sin_raw")
         cos = keep.tile([P, POS_TILES, ROT], F32, name="cos")
         sin = keep.tile([P, POS_TILES, ROT], F32, name="sin")
-        bias_rot = [keep.tile([P, ROT, HEADS_PER_BANK], F32, name="bias_rot%d" % c) for c in range(QK_CHUNKS)]
-        bias_pass = [keep.tile([P, HEADS_PER_BANK, ROT], F32, name="bias_pass%d" % c) for c in range(QK_CHUNKS)]
-        bias_v = [keep.tile([P, BANK], F32, name="bias_v%d" % c) for c in range(CHUNKS - QK_CHUNKS)]
+        bias = [keep.tile([P, BANK], F32, name="bias%d" % c) for c in range(CHUNKS)]
         x_sb = [keep.tile([P, E], BF16, name="x%d" % i) for i in range(TILES)]
         codes = [keep.tile([P, PASSES * P], U32, name="codes%d" % i, align_bytes=64) for i in range(TILES)]
         x_scale = [keep.tile([P, PASSES * P], U8, name="xscale%d" % i, align_bytes=64) for i in range(TILES)]
         w_words = {}
-        x_t, grouped, turned, plain, value, t_cos, t_sin = {}, {}, {}, {}, {}, {}, {}
+        x_t, grouped, turned, value, cos_head, cos_tail, t_sin = {}, {}, {}, {}, {}, {}, {}
 
         def load_x(i):
             nc.sync.dma_start(out=x_sb[i][:], in_=token_rows(x, i))
@@ -99,15 +99,10 @@ def tile_improvedattention_pa_kernel(tc, x, W_qkv_words, W_qkv_scales, b_qkv, si
             row, part = divmod(c, BIAS_CHUNKS)
             acc = psum.tile([P, BANK], F32, name="bias_acc", tag="bank")
             nc.tensor.matmul(acc[:], lhsT=pick[:, row : row + 1].to_broadcast([P, P]), rhs=bias_rows[:, BANK * part : BANK * (part + 1)], start=True, stop=True)
-            if c < QK_CHUNKS:
-                copy(out=bias_rot[c][:], in_=acc[:].rearrange("p (h d) -> p d h", d=D)[:, 0:ROT, :])
-                copy(out=bias_pass[c][:], in_=acc[:].rearrange("p (h d) -> p h d", d=D)[:, :, ROT:D])
-            else:
-                copy(out=bias_v[c - QK_CHUNKS][:], in_=acc[:])
+            copy(out=bias[c][:], in_=acc[:])
 
         def project(i, c):
             if c == 0:
-                plain[i] = work.tile([P, ROT, QK_HEADS], F32, name="u")
                 turned[i] = stage.tile([P, QK_HEADS, D], F32, name="qk")
                 value[i] = stage.tile([P, E], F32, name="v")
             acc = psum.tile([P, BANK], F32, name="acc", tag="bank")
@@ -122,47 +117,43 @@ def tile_improvedattention_pa_kernel(tc, x, W_qkv_words, W_qkv_scales, b_qkv, si
                     stop=(g == PASSES - 1),
                 )
             if c < QK_CHUNKS:
-                heads = slice(HEADS_PER_BANK * c, HEADS_PER_BANK * (c + 1))
-                nc.vector.tensor_tensor(
-                    out=plain[i][:, :, heads],
-                    in0=acc[:].rearrange("p (h d) -> p d h", d=D)[:, 0:ROT, :],
-                    in1=bias_rot[c][:],
-                    op=ALU.add,
-                )
-                nc.vector.tensor_tensor(
-                    out=turned[i][:, heads, ROT:D],
-                    in0=acc[:].rearrange("p (h d) -> p h d", d=D)[:, :, ROT:D],
-                    in1=bias_pass[c][:],
-                    op=ALU.add,
-                )
+                dst = turned[i][:, HEADS_PER_BANK * c : HEADS_PER_BANK * (c + 1), :].rearrange("p h d -> p (h d)")
             else:
-                cv = c - QK_CHUNKS
-                nc.vector.tensor_tensor(out=value[i][:, BANK * cv : BANK * (cv + 1)], in0=acc[:], in1=bias_v[cv][:], op=ALU.add)
+                dst = value[i][:, BANK * (c - QK_CHUNKS) : BANK * (c - QK_CHUNKS + 1)]
+            nc.vector.tensor_tensor(out=dst, in0=acc[:], in1=bias[c][:], op=ALU.add)
 
-        def cos_share(i):
-            t_cos[i] = work.tile([P, ROT, QK_HEADS], F32, name="t_cos")
-            t_sin[i] = work.tile([P, ROT, QK_HEADS], F32, name="t_sin")
-            js = slice(ROT - POOL_COS, ROT)
-            nc.gpsimd.tensor_tensor(
-                out=t_cos[i][:, js, :],
-                in0=plain[i][:, js, :],
-                in1=cos[:, i // B, js].unsqueeze(2).to_broadcast([P, POOL_COS, QK_HEADS]),
+        def halves(i):
+            return turned[i][:, :, 0:ROT].rearrange("p n (h j) -> p h n j", h=2)
+
+        def cos_product(i, engine, j0, j1, name):
+            prod = work.tile([P, 2, QK_HEADS, j1 - j0], F32, name=name)
+            table = cos[:, i // B, :].rearrange("p (h j) -> p h j", h=2)[:, :, j0:j1]
+            engine.tensor_tensor(
+                out=prod[:],
+                in0=halves(i)[:, :, :, j0:j1],
+                in1=table.unsqueeze(2).to_broadcast([P, 2, QK_HEADS, j1 - j0]),
                 op=ALU.mult,
             )
+            return prod
 
-        def rotate(i, half):
+        def rotate(i, a, engine):
             t = i // B
-            for j in range(PAIR * half, PAIR * (half + 1)):
-                mate = (j + PAIR) % ROT
-                if j < ROT - POOL_COS:
-                    nc.scalar.activation(out=t_cos[i][:, j, :], in_=plain[i][:, j, :], func=ACT.Copy, scale=cos[:, t, j : j + 1])
-                nc.scalar.activation(out=t_sin[i][:, j, :], in_=plain[i][:, mate, :], func=ACT.Copy, scale=sin[:, t, j : j + 1])
-            js = slice(PAIR * half, PAIR * (half + 1))
-            nc.gpsimd.tensor_tensor(
-                out=turned[i][:, :, js].rearrange("p n (a j) -> p a n j", j=4),
-                in0=t_cos[i][:, js, :].rearrange("p (a j) n -> p a n j", j=4),
-                in1=t_sin[i][:, js, :].rearrange("p (a j) n -> p a n j", j=4),
-                op=ALU.subtract if half == 0 else ALU.add,
+            if a == 0:
+                t_sin[i] = work.tile([P, 2, PAIR, QK_HEADS], F32, name="t_sin")
+            js = slice(LINE * a, LINE * (a + 1))
+            for h in range(2):
+                for j in range(LINE * a, LINE * (a + 1)):
+                    nc.scalar.activation(
+                        out=t_sin[i][:, h, j, :],
+                        in_=halves(i)[:, 1 - h, :, j],
+                        func=ACT.Copy,
+                        scale=sin[:, t, PAIR * h + j : PAIR * h + j + 1],
+                    )
+            engine.tensor_tensor(
+                out=halves(i)[:, :, :, js],
+                in0=cos_head[i][:, :, :, js] if a < GROUPS - 1 else cos_tail[i][:],
+                in1=t_sin[i][:, :, js, :].rearrange("p h j n -> p h n j"),
+                op=ALU.add,
             )
 
         def store_qk(i):
@@ -192,7 +183,8 @@ def tile_improvedattention_pa_kernel(tc, x, W_qkv_words, W_qkv_scales, b_qkv, si
         for i in range(2, TILES):
             load_x(i)
         nc.scalar.activation(out=cos[:], in_=cos_raw[:], func=ACT.Copy)
-        nc.scalar.activation(out=sin[:], in_=sin_raw[:], func=ACT.Copy)
+        nc.scalar.activation(out=sin[:, :, 0:PAIR], in_=sin_raw[:, :, 0:PAIR], func=ACT.Copy, scale=-1.0)
+        nc.scalar.activation(out=sin[:, :, PAIR:ROT], in_=sin_raw[:, :, PAIR:ROT], func=ACT.Copy)
 
         transpose_x(0)
         group_x(0)
@@ -201,12 +193,16 @@ def tile_improvedattention_pa_kernel(tc, x, W_qkv_words, W_qkv_scales, b_qkv, si
         spread_bias(1, nc.scalar.copy)
 
         for i in range(TILES):
+            last = i == TILES - 1
             ahead = [n for n in (i + 2, i + 3) if i % 2 == 0 and n < TILES]
             for c in range(CHUNKS):
                 if i == 0 and c == QK_CHUNKS:
                     transpose_x(1)
                     group_x(1)
                 project(i, c)
+                if c == QK_CHUNKS - 1:
+                    cos_head[i] = cos_product(i, nc.vector, 0, VEC_COS, "cos_head")
+                    cos_tail[i] = cos_product(i, nc.vector if last else nc.gpsimd, VEC_COS, PAIR, "cos_tail")
                 if i == 0 and c + 2 < CHUNKS:
                     spread_bias(c + 2, nc.scalar.copy)
                 if i == 0 and c == QK_CHUNKS:
@@ -218,9 +214,9 @@ def tile_improvedattention_pa_kernel(tc, x, W_qkv_words, W_qkv_scales, b_qkv, si
             store_v(i)
             for n in ahead:
                 transpose_x(n)
-            cos_share(i)
-            rotate(i, 0)
-            for n in ahead:
-                group_x(n)
-            rotate(i, 1)
+            for a in range(GROUPS):
+                rotate(i, a, nc.vector if last and a >= GROUPS // 2 else nc.gpsimd)
+                if a == GROUPS // 2 - 1:
+                    for n in ahead:
+                        group_x(n)
             store_qk(i)

@@ -30,10 +30,7 @@ TILES = B * POS_TILES
 QK_HEADS = 2 * H
 W_LOADS = [(0, 1), (1, 2), (2, 4), (4, 6)]
 LINE = 4
-GROUPS = PAIR // LINE
-VEC_COS = PAIR - LINE
-BIAS_ROWS = 2
-BIAS_CHUNKS = CHUNKS // BIAS_ROWS
+AHEAD = 3
 
 
 def tile_improvedattention_pa_kernel(tc, x, W_qkv_words, W_qkv_scales, b_qkv, sin_tab, cos_tab, out_0, out_1, out_2):
@@ -53,7 +50,7 @@ def tile_improvedattention_pa_kernel(tc, x, W_qkv_words, W_qkv_scales, b_qkv, si
 
         ident = keep.tile([P, P], F32, name="ident")
         pick = keep.tile([P, 8], BF16, name="pick")
-        bias_rows = keep.tile([P, BIAS_CHUNKS * BANK], BF16, name="bias_rows")
+        bias_rows = keep.tile([P, BANK], BF16, name="bias_rows")
         w_scale = keep.tile([P, PASSES, 3 * E], U8, name="w_scale", align_bytes=64)
         cos_raw = keep.tile([P, POS_TILES, ROT], BF16, name="cos_raw")
         sin_raw = keep.tile([P, POS_TILES, ROT], BF16, name="sin_raw")
@@ -64,7 +61,7 @@ def tile_improvedattention_pa_kernel(tc, x, W_qkv_words, W_qkv_scales, b_qkv, si
         codes = [keep.tile([P, PASSES * P], U32, name="codes%d" % i, align_bytes=64) for i in range(TILES)]
         x_scale = [keep.tile([P, PASSES * P], U8, name="xscale%d" % i, align_bytes=64) for i in range(TILES)]
         w_words = {}
-        x_t, grouped, turned, value, cos_head, cos_tail, t_sin = {}, {}, {}, {}, {}, {}, {}
+        x_t, grouped, turned, value, t_cos, t_sin = {}, {}, {}, {}, {}, {}
 
         def load_x(i):
             nc.sync.dma_start(out=x_sb[i][:], in_=token_rows(x, i))
@@ -96,9 +93,8 @@ def tile_improvedattention_pa_kernel(tc, x, W_qkv_words, W_qkv_scales, b_qkv, si
             nc.vector.quantize_mx(out=codes[i][:].bitcast(E5M2X4), scales=x_scale[i][:], in_=grouped[i][:])
 
         def spread_bias(c, copy):
-            row, part = divmod(c, BIAS_CHUNKS)
             acc = psum.tile([P, BANK], F32, name="bias_acc", tag="bank")
-            nc.tensor.matmul(acc[:], lhsT=pick[:, row : row + 1].to_broadcast([P, P]), rhs=bias_rows[:, BANK * part : BANK * (part + 1)], start=True, stop=True)
+            nc.tensor.matmul(acc[:], lhsT=pick[:, c : c + 1].to_broadcast([P, P]), rhs=bias_rows[:], start=True, stop=True)
             copy(out=bias[c][:], in_=acc[:])
 
         def project(i, c):
@@ -122,43 +118,35 @@ def tile_improvedattention_pa_kernel(tc, x, W_qkv_words, W_qkv_scales, b_qkv, si
                 dst = value[i][:, BANK * (c - QK_CHUNKS) : BANK * (c - QK_CHUNKS + 1)]
             nc.vector.tensor_tensor(out=dst, in0=acc[:], in1=bias[c][:], op=ALU.add)
 
-        def halves(i):
-            return turned[i][:, :, 0:ROT].rearrange("p n (h j) -> p h n j", h=2)
-
-        def cos_product(i, engine, j0, j1, name):
-            prod = work.tile([P, 2, QK_HEADS, j1 - j0], F32, name=name)
-            table = cos[:, i // B, :].rearrange("p (h j) -> p h j", h=2)[:, :, j0:j1]
-            engine.tensor_tensor(
-                out=prod[:],
-                in0=halves(i)[:, :, :, j0:j1],
-                in1=table.unsqueeze(2).to_broadcast([P, 2, QK_HEADS, j1 - j0]),
+        def cos_product(i):
+            t_cos[i] = work.tile([P, QK_HEADS, ROT], F32, name="t_cos")
+            nc.vector.tensor_tensor(
+                out=t_cos[i][:],
+                in0=turned[i][:, :, 0:ROT],
+                in1=cos[:, i // B, :].unsqueeze(1).to_broadcast([P, QK_HEADS, ROT]),
                 op=ALU.mult,
             )
-            return prod
 
-        def rotate(i, a, engine):
-            t = i // B
-            if a == 0:
-                t_sin[i] = work.tile([P, 2, PAIR, QK_HEADS], F32, name="t_sin")
-            js = slice(LINE * a, LINE * (a + 1))
-            for h in range(2):
-                for j in range(LINE * a, LINE * (a + 1)):
-                    nc.scalar.activation(
-                        out=t_sin[i][:, h, j, :],
-                        in_=halves(i)[:, 1 - h, :, j],
-                        func=ACT.Copy,
-                        scale=sin[:, t, PAIR * h + j : PAIR * h + j + 1],
-                    )
-            engine.tensor_tensor(
-                out=halves(i)[:, :, :, js],
-                in0=cos_head[i][:, :, :, js] if a < GROUPS - 1 else cos_tail[i][:],
-                in1=t_sin[i][:, :, js, :].rearrange("p h j n -> p h n j"),
-                op=ALU.add,
-            )
+        def sin_product(i):
+            t_sin[i] = work.tile([P, ROT, QK_HEADS], F32, name="t_sin")
+            for j in range(ROT):
+                nc.scalar.activation(
+                    out=t_sin[i][:, j, :],
+                    in_=turned[i][:, :, (j + PAIR) % ROT],
+                    func=ACT.Copy,
+                    scale=sin[:, i // B, j : j + 1],
+                )
 
-        def store_qk(i):
+        def combine_and_store(i, engine):
             for k in range(2):
-                nc.sync.dma_start(out=token_rows(outs[k], i), in_=turned[i][:, H * k : H * (k + 1), :].rearrange("p h d -> p (h d)"))
+                heads = slice(H * k, H * (k + 1))
+                engine.tensor_tensor(
+                    out=turned[i][:, heads, 0:ROT].rearrange("p n (a j) -> p a n j", j=LINE),
+                    in0=t_cos[i][:, heads, :].rearrange("p n (a j) -> p a n j", j=LINE),
+                    in1=t_sin[i][:, :, heads].rearrange("p (a j) n -> p a n j", j=LINE),
+                    op=ALU.add,
+                )
+                nc.sync.dma_start(out=token_rows(outs[k], i), in_=turned[i][:, heads, :].rearrange("p h d -> p (h d)"))
 
         def store_v(i):
             nc.sync.dma_start(out=token_rows(outs[2], i), in_=value[i][:])
@@ -167,10 +155,11 @@ def tile_improvedattention_pa_kernel(tc, x, W_qkv_words, W_qkv_scales, b_qkv, si
         nc.gpsimd.tensor_copy(out=pick[:], in_=ident[:, 0:8])
         nc.vector.memset(bias_rows[:].bitcast(I32), 0)
         nc.vector.memset(w_scale[:].bitcast(I32), 0)
-        nc.scalar.dma_start(out=bias_rows[0:BIAS_ROWS, :], in_=b_qkv.rearrange("(r n) -> r n", r=BIAS_ROWS))
+        nc.scalar.dma_start(out=bias_rows[0:CHUNKS, :], in_=b_qkv.rearrange("(c n) -> c n", n=BANK))
         nc.scalar.dma_start(out=cos_raw[:], in_=cos_tab.rearrange("(p t) j -> p t j", t=POS_TILES))
         nc.scalar.dma_start(out=sin_raw[:], in_=sin_tab.rearrange("(p t) j -> p t j", t=POS_TILES))
         load_x(0)
+        load_x(1)
         for q in range(4):
             nc.sync.dma_start(
                 out=w_scale[32 * q : 32 * q + 4, :, :].bitcast(I32),
@@ -178,45 +167,44 @@ def tile_improvedattention_pa_kernel(tc, x, W_qkv_words, W_qkv_scales, b_qkv, si
             )
         for c0, c1 in W_LOADS[:3]:
             load_w(c0, c1)
-        load_x(1)
+        load_x(2)
         load_w(*W_LOADS[3])
-        for i in range(2, TILES):
+        for i in range(AHEAD, TILES):
             load_x(i)
         nc.scalar.activation(out=cos[:], in_=cos_raw[:], func=ACT.Copy)
         nc.scalar.activation(out=sin[:, :, 0:PAIR], in_=sin_raw[:, :, 0:PAIR], func=ACT.Copy, scale=-1.0)
         nc.scalar.activation(out=sin[:, :, PAIR:ROT], in_=sin_raw[:, :, PAIR:ROT], func=ACT.Copy)
 
-        transpose_x(0)
-        group_x(0)
-        quantize_x(0)
+        for i in range(2):
+            transpose_x(i)
+            group_x(i)
+            quantize_x(i)
         spread_bias(0, nc.vector.tensor_copy)
-        spread_bias(1, nc.scalar.copy)
+        for c in range(1, 3):
+            spread_bias(c, nc.scalar.copy)
 
         for i in range(TILES):
-            last = i == TILES - 1
-            ahead = [n for n in (i + 2, i + 3) if i % 2 == 0 and n < TILES]
             for c in range(CHUNKS):
-                if i == 0 and c == QK_CHUNKS:
-                    transpose_x(1)
-                    group_x(1)
                 project(i, c)
-                if c == QK_CHUNKS - 1:
-                    cos_head[i] = cos_product(i, nc.vector, 0, VEC_COS, "cos_head")
-                    cos_tail[i] = cos_product(i, nc.vector if last else nc.gpsimd, VEC_COS, PAIR, "cos_tail")
-                if i == 0 and c + 2 < CHUNKS:
-                    spread_bias(c + 2, nc.scalar.copy)
+                if i == 0 and c + 3 < CHUNKS:
+                    spread_bias(c + 3, nc.scalar.copy)
+                if i == 0 and c == QK_CHUNKS - 1:
+                    transpose_x(2)
+                    group_x(2)
+                    cos_product(0)
                 if i == 0 and c == QK_CHUNKS:
-                    quantize_x(1)
-                if i % 2 == 1 and c == 2:
-                    for n in (i + 1, i + 2):
-                        if n < TILES:
-                            quantize_x(n)
+                    quantize_x(2)
+                if i > 0 and c == 1:
+                    if i > 1:
+                        cos_product(i - 1)
+                        if i + 1 < TILES:
+                            quantize_x(i + 1)
+                    combine_and_store(i - 1, nc.gpsimd)
             store_v(i)
-            for n in ahead:
-                transpose_x(n)
-            for a in range(GROUPS):
-                rotate(i, a, nc.vector if last and a >= GROUPS // 2 else nc.gpsimd)
-                if a == GROUPS // 2 - 1:
-                    for n in ahead:
-                        group_x(n)
-            store_qk(i)
+            if i + AHEAD < TILES:
+                transpose_x(i + AHEAD)
+            sin_product(i)
+            if i + AHEAD < TILES:
+                group_x(i + AHEAD)
+        cos_product(TILES - 1)
+        combine_and_store(TILES - 1, nc.vector)

@@ -194,11 +194,11 @@ def tile_improvedattention_pa_kernel(tc, x, W_qkv_words, W_qkv_scales, b_qkv, si
                     cos_product(0)
                 if i == 0 and c == QK_CHUNKS:
                     quantize_x(2)
-                if i > 0 and c == 1:
+                if i > 0 and c == (2 if i + 1 < TILES else 1):
                     if i > 1:
-                        cos_product(i - 1)
                         if i + 1 < TILES:
                             quantize_x(i + 1)
+                        cos_product(i - 1)
                     combine_and_store(i - 1, nc.gpsimd)
             store_v(i)
             if i + AHEAD < TILES:

@@ -118,9 +118,9 @@ def tile_improvedattention_pa_kernel(tc, x, W_qkv_words, W_qkv_scales, b_qkv, si
                 dst = value[i][:, BANK * (c - QK_CHUNKS) : BANK * (c - QK_CHUNKS + 1)]
             nc.vector.tensor_tensor(out=dst, in0=acc[:], in1=bias[c][:], op=ALU.add)
 
-        def cos_product(i):
-            t_cos[i] = work.tile([P, QK_HEADS, ROT], F32, name="t_cos")
-            nc.vector.tensor_tensor(
+        def cos_product(i, engine):
+            t_cos[i] = work.tile([P, QK_HEADS, ROT], F32, name="t_cos", bufs=1)
+            engine.tensor_tensor(
                 out=t_cos[i][:],
                 in0=turned[i][:, :, 0:ROT],
                 in1=cos[:, i // B, :].unsqueeze(1).to_broadcast([P, QK_HEADS, ROT]),
@@ -137,10 +137,10 @@ def tile_improvedattention_pa_kernel(tc, x, W_qkv_words, W_qkv_scales, b_qkv, si
                     scale=sin[:, i // B, j : j + 1],
                 )
 
-        def combine_and_store(i, engine):
+        def combine_and_store(i):
             for k in range(2):
                 heads = slice(H * k, H * (k + 1))
-                engine.tensor_tensor(
+                nc.vector.tensor_tensor(
                     out=turned[i][:, heads, 0:ROT].rearrange("p n (a j) -> p a n j", j=LINE),
                     in0=t_cos[i][:, heads, :].rearrange("p n (a j) -> p a n j", j=LINE),
                     in1=t_sin[i][:, :, heads].rearrange("p (a j) n -> p a n j", j=LINE),
@@ -191,20 +191,20 @@ def tile_improvedattention_pa_kernel(tc, x, W_qkv_words, W_qkv_scales, b_qkv, si
                 if i == 0 and c == QK_CHUNKS - 1:
                     transpose_x(2)
                     group_x(2)
-                    cos_product(0)
+                    cos_product(0, nc.vector)
                 if i == 0 and c == QK_CHUNKS:
                     quantize_x(2)
-                if i > 0 and c == (2 if i + 1 < TILES else 1):
-                    if i > 1:
-                        if i + 1 < TILES:
-                            quantize_x(i + 1)
-                        cos_product(i - 1)
-                    combine_and_store(i - 1, nc.gpsimd)
+                if i > 0 and c == QK_CHUNKS - 1:
+                    if AHEAD <= i + 1 < TILES:
+                        quantize_x(i + 1)
+                    combine_and_store(i - 1)
+                    if i + 1 < TILES:
+                        cos_product(i, nc.gpsimd)
             store_v(i)
             if i + AHEAD < TILES:
                 transpose_x(i + AHEAD)
             sin_product(i)
             if i + AHEAD < TILES:
                 group_x(i + AHEAD)
-        cos_product(TILES - 1)
-        combine_and_store(TILES - 1, nc.vector)
+        cos_product(TILES - 1, nc.vector)
+        combine_and_store(TILES - 1)

from contextlib import ExitStack

import concourse.mybir as mybir
from concourse.masks import make_identity

B, S, H, D = 2, 512, 16, 64
E = H * D
ROT = D // 2
PAIR = ROT // 2
FLOPS = 2 * B * S * E * 3 * E

F32 = mybir.dt.float32
BF16 = mybir.dt.bfloat16
I32 = mybir.dt.int32
U32 = mybir.dt.uint32
U8 = mybir.dt.uint8
E5M2X4 = mybir.dt.float8_e5m2_x4
E2M1X4 = mybir.dt.float4_e2m1fn_x4
ALU = mybir.AluOpType
ACT = mybir.ActivationFunctionType

P = 128
PASSES = E // 512
BANK = 512
CHUNKS = 3 * E // BANK
QK_CHUNKS = 2 * E // BANK
HEADS_PER_BANK = BANK // D
POS_TILES = S // P
TILES = B * POS_TILES
QK_HEADS = 2 * H
W_LOADS = [(0, 1), (1, 2), (2, 4), (4, 6)]
LINE = 4
AHEAD = 3


def tile_improvedattention_pa_kernel(tc, x, W_qkv_words, W_qkv_scales, b_qkv, sin_tab, cos_tab, out_0, out_1, out_2):
    nc = tc.nc

    def token_rows(ap, i):
        return ap[i % B].rearrange("(p t) e -> t p e", t=POS_TILES)[i // B]

    outs = [o.rearrange("b s h d -> b s (h d)") for o in (out_0, out_1, out_2)]

    with ExitStack() as ctx:
        keep = ctx.enter_context(tc.tile_pool(name="keep", bufs=1))
        work = ctx.enter_context(tc.tile_pool(name="work", bufs=3))
        stage = ctx.enter_context(tc.tile_pool(name="stage", bufs=4))
        psum = ctx.enter_context(tc.psum_pool(name="psum", bufs=8))
        ctx.enter_context(tc.manual_schedule())

        ident = keep.tile([P, P], F32, name="ident")
        pick = keep.tile([P, 8], BF16, name="pick")
        bias_rows = keep.tile([P, BANK], BF16, name="bias_rows")
        w_scale = keep.tile([P, PASSES, 3 * E], U8, name="w_scale", align_bytes=64)
        cos_raw = keep.tile([P, POS_TILES, ROT], BF16, name="cos_raw")
        sin_raw = keep.tile([P, POS_TILES, ROT], BF16, name="sin_raw")
        cos = keep.tile([P, POS_TILES, ROT], F32, name="cos")
        sin = keep.tile([P, POS_TILES, ROT], F32, name="sin")
        bias = [keep.tile([P, BANK], F32, name="bias%d" % c) for c in range(CHUNKS)]
        x_sb = [keep.tile([P, E], BF16, name="x%d" % i) for i in range(TILES)]
        codes = [keep.tile([P, PASSES * P], U32, name="codes%d" % i, align_bytes=64) for i in range(TILES)]
        x_scale = [keep.tile([P, PASSES * P], U8, name="xscale%d" % i, align_bytes=64) for i in range(TILES)]
        w_words = {}
        x_t, grouped, turned, value, t_cos, t_sin = {}, {}, {}, {}, {}, {}

        def load_x(i):
            nc.sync.dma_start(out=x_sb[i][:], in_=token_rows(x, i))

        def load_w(c0, c1):
            w = keep.tile([P, PASSES, 2 * BANK * (c1 - c0)], U8, name="w%d" % c0, align_bytes=64)
            src = W_qkv_words[:, :, 2 * BANK * c0 : 2 * BANK * c1].rearrange("g p n -> p g n")
            nc.sync.dma_start(out=w[:].bitcast(I32), in_=src.bitcast(I32))
            for c in range(c0, c1):
                w_words[c] = w[:, :, 2 * BANK * (c - c0) : 2 * BANK * (c - c0 + 1)]

        def transpose_x(i):
            xt = psum.tile([P, PASSES, 2, P], F32, name="xt", tag="bank")
            words = x_sb[i][:].bitcast(F32)
            for g in range(PASSES):
                for u in range(2):
                    nc.tensor.transpose(xt[:, g, u, :], words[:, 256 * g + u : 256 * (g + 1) : 2], ident[:])
            x_t[i] = xt

        def group_x(i):
            gr = work.tile([P, E], BF16, name="gr", align_bytes=64)
            nc.scalar.copy(
                out=gr[:].bitcast(F32).rearrange("p (g r u) -> p g r u", g=PASSES, u=2),
                in_=x_t[i][:].rearrange("p g u r -> p g r u"),
            )
            grouped[i] = gr

        def quantize_x(i):
            nc.vector.quantize_mx(out=codes[i][:].bitcast(E5M2X4), scales=x_scale[i][:], in_=grouped[i][:])

        def spread_bias(c, copy):
            acc = psum.tile([P, BANK], F32, name="bias_acc", tag="bank")
            nc.tensor.matmul(acc[:], lhsT=pick[:, c : c + 1].to_broadcast([P, P]), rhs=bias_rows[:], start=True, stop=True)
            copy(out=bias[c][:], in_=acc[:])

        def project(i, c):
            if c == 0:
                turned[i] = stage.tile([P, QK_HEADS, D], F32, name="qk")
                value[i] = stage.tile([P, E], F32, name="v")
            acc = psum.tile([P, BANK], F32, name="acc", tag="bank")
            for g in range(PASSES):
                nc.tensor.matmul_mx(
                    out=acc[:],
                    lhsT=codes[i][:, P * g : P * (g + 1)].bitcast(E5M2X4),
                    lhsT_scale=x_scale[i][:, P * g : P * (g + 1)],
                    rhs=w_words[c][:, g, :].bitcast(E2M1X4),
                    rhs_scale=w_scale[:, g, BANK * c : BANK * (c + 1)],
                    start=(g == 0),
                    stop=(g == PASSES - 1),
                )
            if c < QK_CHUNKS:
                dst = turned[i][:, HEADS_PER_BANK * c : HEADS_PER_BANK * (c + 1), :].rearrange("p h d -> p (h d)")
            else:
                dst = value[i][:, BANK * (c - QK_CHUNKS) : BANK * (c - QK_CHUNKS + 1)]
            nc.vector.tensor_tensor(out=dst, in0=acc[:], in1=bias[c][:], op=ALU.add)

        def cos_product(i, engine):
            t_cos[i] = work.tile([P, QK_HEADS, ROT], F32, name="t_cos", bufs=1)
            engine.tensor_tensor(
                out=t_cos[i][:],
                in0=turned[i][:, :, 0:ROT],
                in1=cos[:, i // B, :].unsqueeze(1).to_broadcast([P, QK_HEADS, ROT]),
                op=ALU.mult,
            )

        def sin_product(i):
            t_sin[i] = work.tile([P, ROT, QK_HEADS], F32, name="t_sin")
            for j in range(ROT):
                nc.scalar.activation(
                    out=t_sin[i][:, j, :],
                    in_=turned[i][:, :, (j + PAIR) % ROT],
                    func=ACT.Copy,
                    scale=sin[:, i // B, j : j + 1],
                )

        def combine_and_store(i):
            for k in range(2):
                heads = slice(H * k, H * (k + 1))
                nc.vector.tensor_tensor(
                    out=turned[i][:, heads, 0:ROT].rearrange("p n (a j) -> p a n j", j=LINE),
                    in0=t_cos[i][:, heads, :].rearrange("p n (a j) -> p a n j", j=LINE),
                    in1=t_sin[i][:, :, heads].rearrange("p (a j) n -> p a n j", j=LINE),
                    op=ALU.add,
                )
                nc.sync.dma_start(out=token_rows(outs[k], i), in_=turned[i][:, heads, :].rearrange("p h d -> p (h d)"))

        def store_v(i):
            nc.sync.dma_start(out=token_rows(outs[2], i), in_=value[i][:])

        make_identity(nc, ident[:])
        nc.gpsimd.tensor_copy(out=pick[:], in_=ident[:, 0:8])
        nc.vector.memset(bias_rows[:].bitcast(I32), 0)
        nc.vector.memset(w_scale[:].bitcast(I32), 0)
        nc.scalar.dma_start(out=bias_rows[0:CHUNKS, :], in_=b_qkv.rearrange("(c n) -> c n", n=BANK))
        nc.scalar.dma_start(out=cos_raw[:], in_=cos_tab.rearrange("(p t) j -> p t j", t=POS_TILES))
        nc.scalar.dma_start(out=sin_raw[:], in_=sin_tab.rearrange("(p t) j -> p t j", t=POS_TILES))
        load_x(0)
        load_x(1)
        for q in range(4):
            nc.sync.dma_start(
                out=w_scale[32 * q : 32 * q + 4, :, :].bitcast(I32),
                in_=W_qkv_scales[:, 4 * q : 4 * q + 4, :].rearrange("g r n -> r g n").bitcast(I32),
            )
        for c0, c1 in W_LOADS[:3]:
            load_w(c0, c1)
        load_x(2)
        load_w(*W_LOADS[3])
        for i in range(AHEAD, TILES):
            load_x(i)
        nc.scalar.activation(out=cos[:], in_=cos_raw[:], func=ACT.Copy)
        nc.scalar.activation(out=sin[:, :, 0:PAIR], in_=sin_raw[:, :, 0:PAIR], func=ACT.Copy, scale=-1.0)
        nc.scalar.activation(out=sin[:, :, PAIR:ROT], in_=sin_raw[:, :, PAIR:ROT], func=ACT.Copy)

        for i in range(2):
            transpose_x(i)
            group_x(i)
            quantize_x(i)
        spread_bias(0, nc.vector.tensor_copy)
        for c in range(1, 3):
            spread_bias(c, nc.scalar.copy)

        for i in range(TILES):
            for c in range(CHUNKS):
                project(i, c)
                if i == 0 and c + 3 < CHUNKS:
                    spread_bias(c + 3, nc.scalar.copy)
                if i == 0 and c == QK_CHUNKS - 1:
                    transpose_x(2)
                    group_x(2)
                    cos_product(0, nc.vector)
                if i == 0 and c == QK_CHUNKS:
                    quantize_x(2)
                if i > 0 and c == QK_CHUNKS - 1:
                    if AHEAD <= i + 1 < TILES:
                        quantize_x(i + 1)
                    combine_and_store(i - 1)
                    if i + 1 < TILES:
                        cos_product(i, nc.gpsimd)
            store_v(i)
            if i + AHEAD < TILES:
                transpose_x(i + AHEAD)
            sin_product(i)
            if i + AHEAD < TILES:
                group_x(i + AHEAD)
        cos_product(TILES - 1, nc.vector)
        combine_and_store(TILES - 1)
